import numpy as np
import ml_dtypes


def mxq(x, axis, fmt="e4m3"):
    dtype, down = {"e4m3": (ml_dtypes.float8_e4m3fn, 7), "e5m2": (ml_dtypes.float8_e5m2, 14)}[fmt]
    v = np.moveaxis(np.asarray(x, np.float32).astype(ml_dtypes.bfloat16).astype(np.float64), axis, -1)
    blocks = v.reshape(v.shape[:-1] + (-1, 32))
    amax = np.abs(blocks).max(-1, keepdims=True)
    byte = np.maximum(np.where(amax > 0, np.frexp(amax)[1] - 1 + 127, 0) - down, 1)
    scale = np.exp2(byte - 127.0)
    codes = (blocks / scale).astype(np.float32).astype(dtype).astype(np.float64)
    return np.moveaxis((codes * scale).reshape(v.shape), -1, axis)


WIDE = False


def mx_kscale(k):
    if not WIDE:
        return np.ones(k)
    levels = np.array([10, -10, 5, -5, 0])
    if k % 512:
        return np.exp2(np.random.permutation(np.resize(levels, k // 32))).repeat(32)
    a = np.empty((k // 512, 16))
    for p in range(k // 512):
        a[p, :8] = np.random.permutation(np.resize(levels, 8))
        for g in range(8):
            far = levels[np.abs(levels - a[p, g]) >= 10]
            a[p, g + 8] = far[np.random.randint(len(far))]
    return np.exp2(a.ravel()).repeat(32)


BF16 = ml_dtypes.bfloat16


def bf(x):
    return np.asarray(x, np.float32).astype(BF16)


def f64(x):
    return np.asarray(x).astype(np.float64)


B, IN_DIM, LAT, OUT_DIM = 8192, 256, 256, 512
G = IN_DIM + LAT


def sigmoid(v):
    return 1.0 / (1.0 + np.exp(-v))


def setup_inputs():
    s = mx_kscale(G)
    return {
        "x_t": bf(np.random.standard_normal((B, IN_DIM)) * s[:IN_DIM]),
        "h_t": bf(np.random.standard_normal((B, LAT)) * 0.85 * s[IN_DIM:]),
        "Wy": bf(np.random.standard_normal((G, OUT_DIM)) * 0.8 / np.sqrt(G) / s[:, None]),
        "by": bf(np.random.standard_normal(OUT_DIM) * 0.2),
        "Wo": bf(np.random.standard_normal((G, OUT_DIM)) * 0.8 / np.sqrt(G) / s[:, None]),
        "bo": bf(np.random.standard_normal(OUT_DIM) * 0.2),
    }


def reference(x_t, h_t, Wy, by, Wo, bo):
    xq = mxq(np.concatenate([f64(x_t), f64(h_t)], axis=1), 1, "e4m3")
    y_hat = np.tanh((xq @ mxq(f64(Wy), 0, "e4m3")) + f64(by))
    o_t = sigmoid((xq @ mxq(f64(Wo), 0, "e4m3")) + f64(bo))
    return y_hat * o_t

@@ -1,0 +1,279 @@
+from contextlib import ExitStack
+
+import concourse.mybir as mybir
+from concourse.masks import make_identity
+
+FP8X4 = mybir.dt.float8_e4m3fn_x4
+BF16 = mybir.dt.bfloat16
+F32 = mybir.dt.float32
+U32 = mybir.dt.uint32
+U8 = mybir.dt.uint8
+ACT = mybir.ActivationFunctionType
+ALU = mybir.AluOpType
+
+P = 128
+ROWS = 8192
+HALF_K = 256
+N_OUT = 512
+TILES = ROWS // P
+GROUP = 4
+GROUPS = TILES // GROUP
+GROWS = GROUP * P
+BLOCKS = N_OUT // P
+LOAD_CHUNKS = (1, 1, 1, 1, 2, 2, 4, 4)
+FUNCS = (("y", ACT.Tanh), ("o", ACT.Sigmoid))
+
+FLOPS = 2 * ROWS * (2 * HALF_K) * (2 * N_OUT)
+
+
+def tile_gatel0rdcell_pb_t_kernel(tc, x_t, h_t, Wy, by, Wo, bo, out):
+    nc = tc.nc
+    x_v = x_t.rearrange("(p j) k -> p j k", j=TILES)
+    h_v = h_t.rearrange("(p j) k -> p j k", j=TILES)
+    out_v = out.rearrange("(p j) c -> p (j c)", j=TILES)
+
+    with ExitStack() as ctx:
+        const = ctx.enter_context(tc.tile_pool(name="const", bufs=1))
+        stage = ctx.enter_context(tc.tile_pool(name="stage", bufs=3))
+        work = ctx.enter_context(tc.tile_pool(name="work", bufs=4))
+        psum_t = ctx.enter_context(tc.psum_pool(name="psum_t", bufs=4))
+        psum_m = ctx.enter_context(tc.psum_pool(name="psum_m", bufs=4))
+        ctx.enter_context(tc.manual_schedule())
+
+        brow = const.tile([2 * BLOCKS, P], BF16, name="brow")
+        brow32 = const.tile([P, P], F32, name="brow32")
+        bias = const.tile([P, 2 * BLOCKS], F32, name="bias")
+        warm = const.tile([P, 8], F32, name="warm")
+        ident = const.tile([P, P], F32, name="ident")
+        nc.scalar.dma_start(out=brow[0:BLOCKS, :], in_=by.rearrange("(r m) -> r m", r=BLOCKS))
+        nc.scalar.dma_start(out=brow[BLOCKS : 2 * BLOCKS, :], in_=bo.rearrange("(r m) -> r m", r=BLOCKS))
+        nc.vector.memset(warm[:], 0.0)
+        nc.vector.memset(brow32[:], 0.0)
+        make_identity(nc, ident[:])
+        nc.scalar.activation(out=warm[:, 4:8], in_=warm[:, 0:4], func=ACT.Sigmoid)
+
+        x_of = {}
+        w_raw = {}
+
+        def load_rows(first_group, n_groups):
+            rows = n_groups * GROUP
+            lo = first_group * GROUP
+            xh = const.tile([P, rows * 2 * HALF_K], BF16, name="xh%d" % first_group)
+            joined = xh[:].rearrange("p (j k) -> p j k", k=2 * HALF_K)
+            nc.sync.dma_start(out=joined[:, :, 0:HALF_K], in_=x_v[:, lo : lo + rows, :])
+            nc.sync.dma_start(out=joined[:, :, HALF_K : 2 * HALF_K], in_=h_v[:, lo : lo + rows, :])
+            for i in range(n_groups):
+                x_of[first_group + i] = (xh, i)
+
+        def load_w(key, w):
+            raw = const.tile([P, 4 * N_OUT], BF16, name="raw_" + key)
+            nc.sync.dma_start(out=raw[:], in_=w.rearrange("(p t) n -> p (t n)", t=4))
+            w_raw[key] = raw
+
+        load_rows(0, LOAD_CHUNKS[0])
+        load_w("y", Wy)
+        load_w("o", Wo)
+        first = LOAD_CHUNKS[0]
+        for n_groups in LOAD_CHUNKS[1:]:
+            load_rows(first, n_groups)
+            first += n_groups
+
+        banks = {}
+        grouped = {}
+        codes = {}
+        acc = {}
+        gate = {}
+        turned = {}
+        result = {}
+        w_q = {}
+
+        def ok(g):
+            return 0 <= g < GROUPS
+
+        def transposes_in(g, b):
+            xh, i = x_of[g]
+            pt = psum_t.tile([P, 2, 2 * P], F32, name="pt", tag="pt")
+            words = xh[:].bitcast(F32)
+            for u in range(2):
+                for jl in range(2):
+                    j = i * GROUP + 2 * b + jl
+                    nc.tensor.transpose(
+                        pt[:, u, jl * P : (jl + 1) * P], words[:, 2 * P * j + u : 2 * P * (j + 1) : 2], ident[:]
+                    )
+            banks[(g, b)] = pt
+
+        def copy_in(g, b, engine_copy):
+            if g not in grouped:
+                gr = stage.tile([P, 4 * GROWS], BF16, name="gr", tag="gr", align_bytes=64)
+                grouped[g] = gr
+            words = grouped[g][:].bitcast(F32).rearrange("p (n u) -> p n u", u=2)
+            engine_copy(out=words[:, 2 * P * b : 2 * P * (b + 1), :], in_=banks[(g, b)][:].rearrange("p u n -> p n u"))
+
+        def quantise(g):
+            cw = stage.tile([P, GROWS], U32, name="cw", tag="cw", align_bytes=64)
+            cs = stage.tile([P, GROWS], U8, name="cs", tag="cs", align_bytes=64)
+            nc.vector.quantize_mx(out=cw[:].bitcast(FP8X4), scales=cs[:], in_=grouped[g][:])
+            codes[g] = (cw, cs)
+
+        def regroup_w(key, h, engine_copy):
+            gw = const.tile([P, 2 * N_OUT], BF16, name="gw_%s%d" % (key, h), align_bytes=64)
+            half = w_raw[key][:].rearrange("p (t n) -> p t n", t=4)[:, :, h * 2 * P : (h + 1) * 2 * P]
+            engine_copy(
+                out=gw[:].rearrange("p (c i t) -> p c t i", i=4, t=4),
+                in_=half.rearrange("p t (c i) -> p c t i", i=4),
+            )
+            grouped[(key, h)] = gw
+
+        def quantise_w(key, h):
+            cw = const.tile([P, 2 * P], U32, name="wcw_%s%d" % (key, h), align_bytes=64)
+            cs = const.tile([P, 2 * P], U8, name="wcs_%s%d" % (key, h), align_bytes=64)
+            nc.vector.quantize_mx(out=cw[:].bitcast(FP8X4), scales=cs[:], in_=grouped[(key, h)][:])
+            w_q[(key, h)] = (cw, cs)
+
+        def order_of(g, h):
+            blocks = (2 * h, 2 * h + 1)
+            if g == 0:
+                return [(c, f) for f in range(2) for c in blocks]
+            return [(c, f) for c in blocks for f in range(2)]
+
+        def passes(g, h, first=0, n=4):
+            cw, cs = codes[g]
+            for c, f in order_of(g, h)[first : first + n]:
+                wc, ws = w_q[(FUNCS[f][0], h)]
+                lo = (c - 2 * h) * P
+                a = psum_m.tile([P, GROWS], F32, name="acc", tag="acc")
+                nc.tensor.matmul_mx(
+                    out=a[:],
+                    lhsT=wc[:, lo : lo + P].bitcast(FP8X4),
+                    lhsT_scale=ws[:, lo : lo + P],
+                    rhs=cw[:].bitcast(FP8X4),
+                    rhs_scale=cs[:],
+                    start=True,
+                    stop=True,
+                )
+                acc[(g, c, f)] = a
+
+        def activate(g, h):
+            if g not in gate:
+                ty = work.tile([P, BLOCKS * GROWS], F32, name="ty", tag="ty")
+                to = work.tile([P, BLOCKS * GROWS], F32, name="to", tag="to")
+                gate[g] = (ty, to)
+            for c, f in order_of(g, h):
+                nc.scalar.activation(
+                    out=gate[g][f][:, c * GROWS : (c + 1) * GROWS],
+                    in_=acc[(g, c, f)][:],
+                    func=FUNCS[f][1],
+                    bias=bias[:, f * BLOCKS + c : f * BLOCKS + c + 1],
+                )
+
+        def multiply(g, c, n, engine):
+            sl = slice(c * GROWS, (c + n) * GROWS)
+            engine.tensor_tensor(out=gate[g][0][:, sl], in0=gate[g][0][:, sl], in1=gate[g][1][:, sl], op=ALU.mult)
+
+        def transposes_out(g, jl):
+            po = psum_t.tile([P, N_OUT], F32, name="po", tag="pt")
+            for c in range(BLOCKS):
+                lo = c * GROWS + jl * P
+                nc.tensor.transpose(po[:, c * P : (c + 1) * P], gate[g][0][:, lo : lo + P], ident[:])
+            turned[(g, jl)] = po
+
+        def copy_out(g, jl, engine_copy):
+            if g not in result:
+                res = work.tile([P, GROUP * N_OUT], F32, name="res", tag="res")
+                result[g] = res
+            engine_copy(out=result[g][:, jl * N_OUT : (jl + 1) * N_OUT], in_=turned[(g, jl)][:])
+
+        def store(g, jl, n):
+            d0 = (g * GROUP + jl) * N_OUT
+            nc.sync.dma_start(out=out_v[:, d0 : d0 + n * N_OUT], in_=result[g][:, jl * N_OUT : (jl + n) * N_OUT])
+
+        vcopy = nc.vector.tensor_copy
+        scopy = nc.scalar.copy
+
+        nc.vector.tensor_copy(out=brow32[0 : 2 * BLOCKS, :], in_=brow[:])
+        pb = psum_m.tile([P, GROWS], F32, name="acc", tag="acc")
+        nc.tensor.transpose(pb[:, 0:P], brow32[:], ident[:])
+        nc.vector.tensor_copy(out=bias[:], in_=pb[:, 0 : 2 * BLOCKS])
+        transposes_in(0, 0)
+        transposes_in(0, 1)
+        copy_in(0, 0, scopy)
+        copy_in(0, 1, scopy)
+        regroup_w("y", 0, vcopy)
+        quantise_w("y", 0)
+        quantise(0)
+        passes(0, 0, 0, 2)
+        transposes_in(1, 0)
+        transposes_in(1, 1)
+        regroup_w("o", 0, scopy)
+        regroup_w("y", 1, vcopy)
+        quantise_w("o", 0)
+        passes(0, 0, 2, 2)
+        quantise_w("y", 1)
+        regroup_w("o", 1, vcopy)
+        quantise_w("o", 1)
+        copy_in(1, 0, vcopy)
+        copy_in(1, 1, vcopy)
+        quantise(1)
+
+        def tail(t):
+            return t + 2 >= GROUPS
+
+        for t in range(GROUPS + 1):
+            if ok(t):
+                activate(t, 0)
+                if t == GROUPS - 1:
+                    multiply(t, 0, 1, nc.vector)
+                    multiply(t, 1, 1, nc.vector)
+                else:
+                    multiply(t, 0, 2, nc.gpsimd)
+            if ok(t + 2) and t > 0:
+                transposes_in(t + 2, 0)
+            if ok(t - 2) and not tail(t - 1):
+                transposes_out(t - 2, 2)
+                transposes_out(t - 2, 3)
+            if ok(t):
+                passes(t, 1)
+            if ok(t + 2) and t > 0:
+                copy_in(t + 2, 0, vcopy)
+            if ok(t - 2) and not tail(t - 1):
+                copy_out(t - 2, 2, vcopy)
+                copy_out(t - 2, 3, vcopy)
+                store(t - 2, 0, GROUP)
+            if ok(t):
+                activate(t, 1)
+                multiply(t, 2, 1, nc.gpsimd)
+            if ok(t + 2):
+                if t == 0:
+                    transposes_in(t + 2, 0)
+                transposes_in(t + 2, 1)
+            if ok(t - 1):
+                for jl in range(GROUP if tail(t) else 2):
+                    transposes_out(t - 1, jl)
+            if ok(t + 1):
+                passes(t + 1, 0)
+            if ok(t + 2):
+                if t == 0:
+                    copy_in(t + 2, 0, vcopy)
+                copy_in(t + 2, 1, vcopy)
+            if ok(t - 1):
+                if t == GROUPS:
+                    for jl in range(GROUP):
+                        copy_out(t - 1, jl, scopy if jl % 2 else vcopy)
+                        store(t - 1, jl, 1)
+                elif t == GROUPS - 1:
+                    copy_out(t - 1, 0, vcopy)
+                    copy_out(t - 1, 1, vcopy)
+                    store(t - 1, 0, 2)
+                    multiply(t, 3, 1, nc.vector)
+                    copy_out(t - 1, 2, scopy)
+                    copy_out(t - 1, 3, scopy)
+                    store(t - 1, 2, 2)
+                else:
+                    for jl in range(GROUP if tail(t) else 2):
+                        copy_out(t - 1, jl, vcopy)
+                    if tail(t):
+                        store(t - 1, 0, GROUP)
+            if ok(t + 2):
+                quantise(t + 2)
+            if ok(t) and t < GROUPS - 1:
+                multiply(t, 3, 1, nc.gpsimd if t == 0 else nc.vector)

@@ -225,7 +225,8 @@ def tile_gatel0rdcell_pb_t_kernel(tc, x_t, h_t, Wy, by, Wo, bo, out):
                     multiply(t, 0, 1, nc.vector)
                     multiply(t, 1, 1, nc.vector)
                 else:
-                    multiply(t, 0, 2, nc.gpsimd)
+                    multiply(t, 0, 1, nc.gpsimd)
+                    multiply(t, 1, 1, nc.gpsimd)
             if ok(t + 2) and t > 0:
                 transposes_in(t + 2, 0)
             if ok(t - 2) and not tail(t - 1):

@@ -65,14 +65,20 @@ def tile_gatel0rdcell_pb_t_kernel(tc, x_t, h_t, Wy, by, Wo, bo, out):
             for i in range(n_groups):
                 x_of[first_group + i] = (xh, i)
 
-        def load_w(key, w):
-            raw = const.tile([P, 4 * N_OUT], BF16, name="raw_" + key)
-            nc.sync.dma_start(out=raw[:], in_=w.rearrange("(p t) n -> p (t n)", t=4))
-            w_raw[key] = raw
+        def load_w(key, w, h):
+            if h == 0:
+                raw = const.tile([P, 4 * N_OUT], BF16, name="raw_" + key)
+                w_raw[key] = raw
+            cols = slice(h * 2 * P, (h + 1) * 2 * P)
+            nc.sync.dma_start(
+                out=w_raw[key][:].rearrange("p (t n) -> p t n", t=4)[:, :, cols],
+                in_=w.rearrange("(p t) n -> p t n", t=4)[:, :, cols],
+            )
 
         load_rows(0, LOAD_CHUNKS[0])
-        load_w("y", Wy)
-        load_w("o", Wo)
+        for h in range(2):
+            load_w("y", Wy, h)
+            load_w("o", Wo, h)
         first = LOAD_CHUNKS[0]
         for n_groups in LOAD_CHUNKS[1:]:
             load_rows(first, n_groups)
@@ -190,16 +196,16 @@ def tile_gatel0rdcell_pb_t_kernel(tc, x_t, h_t, Wy, by, Wo, bo, out):
         vcopy = nc.vector.tensor_copy
         scopy = nc.scalar.copy
 
+        transposes_in(0, 0)
+        transposes_in(0, 1)
         nc.vector.tensor_copy(out=brow32[0 : 2 * BLOCKS, :], in_=brow[:])
+        regroup_w("y", 0, vcopy)
+        copy_in(0, 0, vcopy)
+        copy_in(0, 1, scopy)
+        quantise_w("y", 0)
         pb = psum_m.tile([P, GROWS], F32, name="acc", tag="acc")
         nc.tensor.transpose(pb[:, 0:P], brow32[:], ident[:])
         nc.vector.tensor_copy(out=bias[:], in_=pb[:, 0 : 2 * BLOCKS])
-        transposes_in(0, 0)
-        transposes_in(0, 1)
-        copy_in(0, 0, scopy)
-        copy_in(0, 1, scopy)
-        regroup_w("y", 0, vcopy)
-        quantise_w("y", 0)
         quantise(0)
         passes(0, 0, 0, 2)
         transposes_in(1, 0)
@@ -215,66 +221,130 @@ def tile_gatel0rdcell_pb_t_kernel(tc, x_t, h_t, Wy, by, Wo, bo, out):
         copy_in(1, 1, vcopy)
         quantise(1)
 
-        def tail(t):
-            return t + 2 >= GROUPS
+        LAST = GROUPS - 1
+        HROWS = GROWS // 2
 
-        for t in range(GROUPS + 1):
-            if ok(t):
-                activate(t, 0)
-                if t == GROUPS - 1:
-                    multiply(t, 0, 1, nc.vector)
-                    multiply(t, 1, 1, nc.vector)
-                else:
-                    multiply(t, 0, 1, nc.gpsimd)
-                    multiply(t, 1, 1, nc.gpsimd)
+        def half_passes(r, blocks):
+            cw, cs = codes[LAST]
+            cols = slice(r * HROWS, (r + 1) * HROWS)
+            for c in blocks:
+                a = psum_m.tile([P, 2, HROWS], F32, name="acc", tag="acc")
+                for f in range(2):
+                    wc, ws = w_q[(FUNCS[f][0], c // 2)]
+                    lo = (c % 2) * P
+                    nc.tensor.matmul_mx(
+                        out=a[:, f, :],
+                        lhsT=wc[:, lo : lo + P].bitcast(FP8X4),
+                        lhsT_scale=ws[:, lo : lo + P],
+                        rhs=cw[:, cols].bitcast(FP8X4),
+                        rhs_scale=cs[:, cols],
+                        start=True,
+                        stop=True,
+                    )
+                acc[(r, c)] = a
+
+        def half_activate(r, c):
+            if LAST not in gate:
+                ty = work.tile([P, BLOCKS * GROWS], F32, name="ty", tag="ty")
+                to = work.tile([P, BLOCKS * GROWS], F32, name="to", tag="to")
+                gate[LAST] = (ty, to)
+            lo = c * GROWS + r * HROWS
+            for f in range(2):
+                nc.scalar.activation(
+                    out=gate[LAST][f][:, lo : lo + HROWS],
+                    in_=acc[(r, c)][:, f, :],
+                    func=FUNCS[f][1],
+                    bias=bias[:, f * BLOCKS + c : f * BLOCKS + c + 1],
+                )
+
+        def half_multiply(r, c, engine):
+            sl = slice(c * GROWS + r * HROWS, c * GROWS + (r + 1) * HROWS)
+            ty, to = gate[LAST]
+            engine.tensor_tensor(out=ty[:, sl], in0=ty[:, sl], in1=to[:, sl], op=ALU.mult)
+
+        for t in range(LAST):
+            activate(t, 0)
+            multiply(t, 0, 2, nc.gpsimd)
             if ok(t + 2) and t > 0:
                 transposes_in(t + 2, 0)
-            if ok(t - 2) and not tail(t - 1):
-                transposes_out(t - 2, 2)
-                transposes_out(t - 2, 3)
-            if ok(t):
-                passes(t, 1)
+            outs = [(t - 2, 2), (t - 2, 3)] if ok(t - 2) else []
+            for g, jl in outs:
+                transposes_out(g, jl)
+            passes(t, 1)
             if ok(t + 2) and t > 0:
                 copy_in(t + 2, 0, vcopy)
-            if ok(t - 2) and not tail(t - 1):
-                copy_out(t - 2, 2, vcopy)
-                copy_out(t - 2, 3, vcopy)
+            for g, jl in outs:
+                copy_out(g, jl, vcopy)
+            if outs:
                 store(t - 2, 0, GROUP)
-            if ok(t):
-                activate(t, 1)
-                multiply(t, 2, 1, nc.gpsimd)
+            activate(t, 1)
+            multiply(t, 2, 1, nc.gpsimd)
             if ok(t + 2):
                 if t == 0:
                     transposes_in(t + 2, 0)
                 transposes_in(t + 2, 1)
-            if ok(t - 1):
-                for jl in range(GROUP if tail(t) else 2):
-                    transposes_out(t - 1, jl)
-            if ok(t + 1):
+            outs = [(t - 1, jl) for jl in range(GROUP if t == LAST - 1 else 2)] if t else []
+            for g, jl in outs:
+                transposes_out(g, jl)
+            if t + 1 < LAST:
                 passes(t + 1, 0)
+            else:
+                half_passes(0, (0, 1))
             if ok(t + 2):
                 if t == 0:
                     copy_in(t + 2, 0, vcopy)
                 copy_in(t + 2, 1, vcopy)
-            if ok(t - 1):
-                if t == GROUPS:
-                    for jl in range(GROUP):
-                        copy_out(t - 1, jl, scopy if jl % 2 else vcopy)
-                        store(t - 1, jl, 1)
-                elif t == GROUPS - 1:
-                    copy_out(t - 1, 0, vcopy)
-                    copy_out(t - 1, 1, vcopy)
-                    store(t - 1, 0, 2)
-                    multiply(t, 3, 1, nc.vector)
-                    copy_out(t - 1, 2, scopy)
-                    copy_out(t - 1, 3, scopy)
-                    store(t - 1, 2, 2)
-                else:
-                    for jl in range(GROUP if tail(t) else 2):
-                        copy_out(t - 1, jl, vcopy)
-                    if tail(t):
-                        store(t - 1, 0, GROUP)
+            for g, jl in outs:
+                copy_out(g, jl, vcopy)
+            if t == LAST - 1:
+                store(t - 1, 0, GROUP)
             if ok(t + 2):
                 quantise(t + 2)
-            if ok(t) and t < GROUPS - 1:
-                multiply(t, 3, 1, nc.gpsimd if t == 0 else nc.vector)
+            multiply(t, 3, 1, nc.gpsimd if t == 0 else nc.vector)
+
+        res = work.tile([P, GROUP * N_OUT], F32, name="res", tag="res")
+        rows = res[:].rearrange("p (j n) -> p j n", j=GROUP)
+        rows_out = out_v[:, LAST * GROUP * N_OUT : GROUPS * GROUP * N_OUT].rearrange("p (j n) -> p j n", j=GROUP)
+
+        def turn_blocks(tiles, blocks, name):
+            po = psum_t.tile([P, len(tiles), len(blocks) * P], F32, name=name, tag="pt")
+            for i, jl in enumerate(tiles):
+                for b, c in enumerate(blocks):
+                    lo = c * GROWS + jl * P
+                    nc.tensor.transpose(po[:, i, b * P : (b + 1) * P], gate[LAST][0][:, lo : lo + P], ident[:])
+            return po
+
+        def finish(tiles, blocks, po, engine_copy):
+            js = slice(tiles[0], tiles[-1] + 1)
+            cols = slice(blocks[0] * P, (blocks[-1] + 1) * P)
+            engine_copy(out=rows[:, js, cols], in_=po[:])
+            nc.sync.dma_start(out=rows_out[:, js, cols], in_=rows[:, js, cols])
+
+        for c in range(2):
+            half_activate(0, c)
+            half_multiply(0, c, nc.gpsimd)
+        half_passes(0, (2, 3))
+        for jl in (0, 1):
+            transposes_out(LAST - 1, jl)
+        half_passes(1, (0, 1))
+        for jl in (0, 1):
+            copy_out(LAST - 1, jl, vcopy)
+        store(LAST - 1, 0, 2)
+        for c in range(2, BLOCKS):
+            half_activate(0, c)
+            half_multiply(0, c, nc.gpsimd)
+        for jl in (2, 3):
+            transposes_out(LAST - 1, jl)
+        half_passes(1, (2, 3))
+        for jl in (2, 3):
+            copy_out(LAST - 1, jl, vcopy)
+        store(LAST - 1, 2, 2)
+        for c in range(BLOCKS):
+            half_activate(1, c)
+            half_multiply(1, c, nc.vector if c else nc.gpsimd)
+            if c == 1:
+                finish((1,), (0, 1, 2, 3), turn_blocks((1,), (0, 1, 2, 3), "po"), vcopy)
+        finish((0,), (0, 1, 2, 3), turn_blocks((0,), (0, 1, 2, 3), "po"), scopy)
+        for jl, engine_copy in ((2, scopy), (3, vcopy)):
+            finish((jl,), (0, 1, 2), turn_blocks((jl,), (0, 1, 2), "po"), engine_copy)
+        finish((2, 3), (3,), turn_blocks((2, 3), (3,), "po"), scopy)

from contextlib import ExitStack

import concourse.mybir as mybir
from concourse.masks import make_identity

FP8X4 = mybir.dt.float8_e4m3fn_x4
BF16 = mybir.dt.bfloat16
F32 = mybir.dt.float32
U32 = mybir.dt.uint32
U8 = mybir.dt.uint8
ACT = mybir.ActivationFunctionType
ALU = mybir.AluOpType

P = 128
ROWS = 8192
HALF_K = 256
N_OUT = 512
TILES = ROWS // P
GROUP = 4
GROUPS = TILES // GROUP
GROWS = GROUP * P
BLOCKS = N_OUT // P
LOAD_CHUNKS = (1, 1, 1, 1, 2, 2, 4, 4)
FUNCS = (("y", ACT.Tanh), ("o", ACT.Sigmoid))

FLOPS = 2 * ROWS * (2 * HALF_K) * (2 * N_OUT)


def tile_gatel0rdcell_pb_t_kernel(tc, x_t, h_t, Wy, by, Wo, bo, out):
    nc = tc.nc
    x_v = x_t.rearrange("(p j) k -> p j k", j=TILES)
    h_v = h_t.rearrange("(p j) k -> p j k", j=TILES)
    out_v = out.rearrange("(p j) c -> p (j c)", j=TILES)

    with ExitStack() as ctx:
        const = ctx.enter_context(tc.tile_pool(name="const", bufs=1))
        stage = ctx.enter_context(tc.tile_pool(name="stage", bufs=3))
        work = ctx.enter_context(tc.tile_pool(name="work", bufs=4))
        psum_t = ctx.enter_context(tc.psum_pool(name="psum_t", bufs=4))
        psum_m = ctx.enter_context(tc.psum_pool(name="psum_m", bufs=4))
        ctx.enter_context(tc.manual_schedule())

        brow = const.tile([2 * BLOCKS, P], BF16, name="brow")
        brow32 = const.tile([P, P], F32, name="brow32")
        bias = const.tile([P, 2 * BLOCKS], F32, name="bias")
        warm = const.tile([P, 8], F32, name="warm")
        ident = const.tile([P, P], F32, name="ident")
        nc.scalar.dma_start(out=brow[0:BLOCKS, :], in_=by.rearrange("(r m) -> r m", r=BLOCKS))
        nc.scalar.dma_start(out=brow[BLOCKS : 2 * BLOCKS, :], in_=bo.rearrange("(r m) -> r m", r=BLOCKS))
        nc.vector.memset(warm[:], 0.0)
        nc.vector.memset(brow32[:], 0.0)
        make_identity(nc, ident[:])
        nc.scalar.activation(out=warm[:, 4:8], in_=warm[:, 0:4], func=ACT.Sigmoid)

        x_of = {}
        w_raw = {}

        def load_rows(first_group, n_groups):
            rows = n_groups * GROUP
            lo = first_group * GROUP
            xh = const.tile([P, rows * 2 * HALF_K], BF16, name="xh%d" % first_group)
            joined = xh[:].rearrange("p (j k) -> p j k", k=2 * HALF_K)
            nc.sync.dma_start(out=joined[:, :, 0:HALF_K], in_=x_v[:, lo : lo + rows, :])
            nc.sync.dma_start(out=joined[:, :, HALF_K : 2 * HALF_K], in_=h_v[:, lo : lo + rows, :])
            for i in range(n_groups):
                x_of[first_group + i] = (xh, i)

        def load_w(key, w, h):
            if h == 0:
                raw = const.tile([P, 4 * N_OUT], BF16, name="raw_" + key)
                w_raw[key] = raw
            cols = slice(h * 2 * P, (h + 1) * 2 * P)
            nc.sync.dma_start(
                out=w_raw[key][:].rearrange("p (t n) -> p t n", t=4)[:, :, cols],
                in_=w.rearrange("(p t) n -> p t n", t=4)[:, :, cols],
            )

        load_rows(0, LOAD_CHUNKS[0])
        for h in range(2):
            load_w("y", Wy, h)
            load_w("o", Wo, h)
        first = LOAD_CHUNKS[0]
        for n_groups in LOAD_CHUNKS[1:]:
            load_rows(first, n_groups)
            first += n_groups

        banks = {}
        grouped = {}
        codes = {}
        acc = {}
        gate = {}
        turned = {}
        result = {}
        w_q = {}

        def ok(g):
            return 0 <= g < GROUPS

        def transposes_in(g, b):
            xh, i = x_of[g]
            pt = psum_t.tile([P, 2, 2 * P], F32, name="pt", tag="pt")
            words = xh[:].bitcast(F32)
            for u in range(2):
                for jl in range(2):
                    j = i * GROUP + 2 * b + jl
                    nc.tensor.transpose(
                        pt[:, u, jl * P : (jl + 1) * P], words[:, 2 * P * j + u : 2 * P * (j + 1) : 2], ident[:]
                    )
            banks[(g, b)] = pt

        def copy_in(g, b, engine_copy):
            if g not in grouped:
                gr = stage.tile([P, 4 * GROWS], BF16, name="gr", tag="gr", align_bytes=64)
                grouped[g] = gr
            words = grouped[g][:].bitcast(F32).rearrange("p (n u) -> p n u", u=2)
            engine_copy(out=words[:, 2 * P * b : 2 * P * (b + 1), :], in_=banks[(g, b)][:].rearrange("p u n -> p n u"))

        def quantise(g):
            cw = stage.tile([P, GROWS], U32, name="cw", tag="cw", align_bytes=64)
            cs = stage.tile([P, GROWS], U8, name="cs", tag="cs", align_bytes=64)
            nc.vector.quantize_mx(out=cw[:].bitcast(FP8X4), scales=cs[:], in_=grouped[g][:])
            codes[g] = (cw, cs)

        def regroup_w(key, h, engine_copy):
            gw = const.tile([P, 2 * N_OUT], BF16, name="gw_%s%d" % (key, h), align_bytes=64)
            half = w_raw[key][:].rearrange("p (t n) -> p t n", t=4)[:, :, h * 2 * P : (h + 1) * 2 * P]
            engine_copy(
                out=gw[:].rearrange("p (c i t) -> p c t i", i=4, t=4),
                in_=half.rearrange("p t (c i) -> p c t i", i=4),
            )
            grouped[(key, h)] = gw

        def quantise_w(key, h):
            cw = const.tile([P, 2 * P], U32, name="wcw_%s%d" % (key, h), align_bytes=64)
            cs = const.tile([P, 2 * P], U8, name="wcs_%s%d" % (key, h), align_bytes=64)
            nc.vector.quantize_mx(out=cw[:].bitcast(FP8X4), scales=cs[:], in_=grouped[(key, h)][:])
            w_q[(key, h)] = (cw, cs)

        def order_of(g, h):
            blocks = (2 * h, 2 * h + 1)
            if g == 0:
                return [(c, f) for f in range(2) for c in blocks]
            return [(c, f) for c in blocks for f in range(2)]

        def passes(g, h, first=0, n=4):
            cw, cs = codes[g]
            for c, f in order_of(g, h)[first : first + n]:
                wc, ws = w_q[(FUNCS[f][0], h)]
                lo = (c - 2 * h) * P
                a = psum_m.tile([P, GROWS], F32, name="acc", tag="acc")
                nc.tensor.matmul_mx(
                    out=a[:],
                    lhsT=wc[:, lo : lo + P].bitcast(FP8X4),
                    lhsT_scale=ws[:, lo : lo + P],
                    rhs=cw[:].bitcast(FP8X4),
                    rhs_scale=cs[:],
                    start=True,
                    stop=True,
                )
                acc[(g, c, f)] = a

        def activate(g, h):
            if g not in gate:
                ty = work.tile([P, BLOCKS * GROWS], F32, name="ty", tag="ty")
                to = work.tile([P, BLOCKS * GROWS], F32, name="to", tag="to")
                gate[g] = (ty, to)
            for c, f in order_of(g, h):
                nc.scalar.activation(
                    out=gate[g][f][:, c * GROWS : (c + 1) * GROWS],
                    in_=acc[(g, c, f)][:],
                    func=FUNCS[f][1],
                    bias=bias[:, f * BLOCKS + c : f * BLOCKS + c + 1],
                )

        def multiply(g, c, n, engine):
            sl = slice(c * GROWS, (c + n) * GROWS)
            engine.tensor_tensor(out=gate[g][0][:, sl], in0=gate[g][0][:, sl], in1=gate[g][1][:, sl], op=ALU.mult)

        def transposes_out(g, jl):
            po = psum_t.tile([P, N_OUT], F32, name="po", tag="pt")
            for c in range(BLOCKS):
                lo = c * GROWS + jl * P
                nc.tensor.transpose(po[:, c * P : (c + 1) * P], gate[g][0][:, lo : lo + P], ident[:])
            turned[(g, jl)] = po

        def copy_out(g, jl, engine_copy):
            if g not in result:
                res = work.tile([P, GROUP * N_OUT], F32, name="res", tag="res")
                result[g] = res
            engine_copy(out=result[g][:, jl * N_OUT : (jl + 1) * N_OUT], in_=turned[(g, jl)][:])

        def store(g, jl, n):
            d0 = (g * GROUP + jl) * N_OUT
            nc.sync.dma_start(out=out_v[:, d0 : d0 + n * N_OUT], in_=result[g][:, jl * N_OUT : (jl + n) * N_OUT])

        vcopy = nc.vector.tensor_copy
        scopy = nc.scalar.copy

        transposes_in(0, 0)
        transposes_in(0, 1)
        nc.vector.tensor_copy(out=brow32[0 : 2 * BLOCKS, :], in_=brow[:])
        regroup_w("y", 0, vcopy)
        copy_in(0, 0, vcopy)
        copy_in(0, 1, scopy)
        quantise_w("y", 0)
        pb = psum_m.tile([P, GROWS], F32, name="acc", tag="acc")
        nc.tensor.transpose(pb[:, 0:P], brow32[:], ident[:])
        nc.vector.tensor_copy(out=bias[:], in_=pb[:, 0 : 2 * BLOCKS])
        quantise(0)
        passes(0, 0, 0, 2)
        transposes_in(1, 0)
        transposes_in(1, 1)
        regroup_w("o", 0, scopy)
        regroup_w("y", 1, vcopy)
        quantise_w("o", 0)
        passes(0, 0, 2, 2)
        quantise_w("y", 1)
        regroup_w("o", 1, vcopy)
        quantise_w("o", 1)
        copy_in(1, 0, vcopy)
        copy_in(1, 1, vcopy)
        quantise(1)

        LAST = GROUPS - 1
        HROWS = GROWS // 2

        def half_passes(r, blocks):
            cw, cs = codes[LAST]
            cols = slice(r * HROWS, (r + 1) * HROWS)
            for c in blocks:
                a = psum_m.tile([P, 2, HROWS], F32, name="acc", tag="acc")
                for f in range(2):
                    wc, ws = w_q[(FUNCS[f][0], c // 2)]
                    lo = (c % 2) * P
                    nc.tensor.matmul_mx(
                        out=a[:, f, :],
                        lhsT=wc[:, lo : lo + P].bitcast(FP8X4),
                        lhsT_scale=ws[:, lo : lo + P],
                        rhs=cw[:, cols].bitcast(FP8X4),
                        rhs_scale=cs[:, cols],
                        start=True,
                        stop=True,
                    )
                acc[(r, c)] = a

        def half_activate(r, c):
            if LAST not in gate:
                ty = work.tile([P, BLOCKS * GROWS], F32, name="ty", tag="ty")
                to = work.tile([P, BLOCKS * GROWS], F32, name="to", tag="to")
                gate[LAST] = (ty, to)
            lo = c * GROWS + r * HROWS
            for f in range(2):
                nc.scalar.activation(
                    out=gate[LAST][f][:, lo : lo + HROWS],
                    in_=acc[(r, c)][:, f, :],
                    func=FUNCS[f][1],
                    bias=bias[:, f * BLOCKS + c : f * BLOCKS + c + 1],
                )

        def half_multiply(r, c, engine):
            sl = slice(c * GROWS + r * HROWS, c * GROWS + (r + 1) * HROWS)
            ty, to = gate[LAST]
            engine.tensor_tensor(out=ty[:, sl], in0=ty[:, sl], in1=to[:, sl], op=ALU.mult)

        for t in range(LAST):
            activate(t, 0)
            multiply(t, 0, 2, nc.gpsimd)
            if ok(t + 2) and t > 0:
                transposes_in(t + 2, 0)
            outs = [(t - 2, 2), (t - 2, 3)] if ok(t - 2) else []
            for g, jl in outs:
                transposes_out(g, jl)
            passes(t, 1)
            if ok(t + 2) and t > 0:
                copy_in(t + 2, 0, vcopy)
            for g, jl in outs:
                copy_out(g, jl, vcopy)
            if outs:
                store(t - 2, 0, GROUP)
            activate(t, 1)
            multiply(t, 2, 1, nc.gpsimd)
            if ok(t + 2):
                if t == 0:
                    transposes_in(t + 2, 0)
                transposes_in(t + 2, 1)
            outs = [(t - 1, jl) for jl in range(GROUP if t == LAST - 1 else 2)] if t else []
            for g, jl in outs:
                transposes_out(g, jl)
            if t + 1 < LAST:
                passes(t + 1, 0)
            else:
                half_passes(0, (0, 1))
            if ok(t + 2):
                if t == 0:
                    copy_in(t + 2, 0, vcopy)
                copy_in(t + 2, 1, vcopy)
            for g, jl in outs:
                copy_out(g, jl, vcopy)
            if t == LAST - 1:
                store(t - 1, 0, GROUP)
            if ok(t + 2):
                quantise(t + 2)
            multiply(t, 3, 1, nc.gpsimd if t == 0 else nc.vector)

        res = work.tile([P, GROUP * N_OUT], F32, name="res", tag="res")
        rows = res[:].rearrange("p (j n) -> p j n", j=GROUP)
        rows_out = out_v[:, LAST * GROUP * N_OUT : GROUPS * GROUP * N_OUT].rearrange("p (j n) -> p j n", j=GROUP)

        def turn_blocks(tiles, blocks, name):
            po = psum_t.tile([P, len(tiles), len(blocks) * P], F32, name=name, tag="pt")
            for i, jl in enumerate(tiles):
                for b, c in enumerate(blocks):
                    lo = c * GROWS + jl * P
                    nc.tensor.transpose(po[:, i, b * P : (b + 1) * P], gate[LAST][0][:, lo : lo + P], ident[:])
            return po

        def finish(tiles, blocks, po, engine_copy):
            js = slice(tiles[0], tiles[-1] + 1)
            cols = slice(blocks[0] * P, (blocks[-1] + 1) * P)
            engine_copy(out=rows[:, js, cols], in_=po[:])
            nc.sync.dma_start(out=rows_out[:, js, cols], in_=rows[:, js, cols])

        for c in range(2):
            half_activate(0, c)
            half_multiply(0, c, nc.gpsimd)
        half_passes(0, (2, 3))
        for jl in (0, 1):
            transposes_out(LAST - 1, jl)
        half_passes(1, (0, 1))
        for jl in (0, 1):
            copy_out(LAST - 1, jl, vcopy)
        store(LAST - 1, 0, 2)
        for c in range(2, BLOCKS):
            half_activate(0, c)
            half_multiply(0, c, nc.gpsimd)
        for jl in (2, 3):
            transposes_out(LAST - 1, jl)
        half_passes(1, (2, 3))
        for jl in (2, 3):
            copy_out(LAST - 1, jl, vcopy)
        store(LAST - 1, 2, 2)
        for c in range(BLOCKS):
            half_activate(1, c)
            half_multiply(1, c, nc.vector if c else nc.gpsimd)
            if c == 1:
                finish((1,), (0, 1, 2, 3), turn_blocks((1,), (0, 1, 2, 3), "po"), vcopy)
        finish((0,), (0, 1, 2, 3), turn_blocks((0,), (0, 1, 2, 3), "po"), scopy)
        for jl, engine_copy in ((2, scopy), (3, vcopy)):
            finish((jl,), (0, 1, 2), turn_blocks((jl,), (0, 1, 2), "po"), engine_copy)
        finish((2, 3), (3,), turn_blocks((2, 3), (3,), "po"), scopy)
